import numpy as np
import ml_dtypes


def mxq(x, axis, fmt="e4m3"):
    dtype, down = {"e4m3": (ml_dtypes.float8_e4m3fn, 7), "e5m2": (ml_dtypes.float8_e5m2, 14)}[fmt]
    v = np.moveaxis(np.asarray(x, np.float32).astype(ml_dtypes.bfloat16).astype(np.float64), axis, -1)
    blocks = v.reshape(v.shape[:-1] + (-1, 32))
    amax = np.abs(blocks).max(-1, keepdims=True)
    byte = np.maximum(np.where(amax > 0, np.frexp(amax)[1] - 1 + 127, 0) - down, 1)
    scale = np.exp2(byte - 127.0)
    codes = (blocks / scale).astype(np.float32).astype(dtype).astype(np.float64)
    return np.moveaxis((codes * scale).reshape(v.shape), -1, axis)


WIDE = False


def mx_kscale(k):
    if not WIDE:
        return np.ones(k)
    levels = np.array([10, -10, 5, -5, 0])
    if k % 512:
        return np.exp2(np.random.permutation(np.resize(levels, k // 32))).repeat(32)
    a = np.empty((k // 512, 16))
    for p in range(k // 512):
        a[p, :8] = np.random.permutation(np.resize(levels, 8))
        for g in range(8):
            far = levels[np.abs(levels - a[p, g]) >= 10]
            a[p, g + 8] = far[np.random.randint(len(far))]
    return np.exp2(a.ravel()).repeat(32)


BF16 = ml_dtypes.bfloat16


def bf(x):
    return np.asarray(x, np.float32).astype(BF16)


def f64(x):
    return np.asarray(x).astype(np.float64)


B, S, D, C = 8, 512, 256, 512


def setup_inputs():
    s = mx_kscale(S)
    a = D ** -0.25
    return {"q_rot": bf(np.random.standard_normal((B, S, D)) * a),
            "k_rot": bf(np.random.standard_normal((B, S, D)) * a * s[:, None]),
            "v": bf(np.random.standard_normal((B, S, D)) * 0.5 / s[:, None]),
            "gamma": bf(1.0 - 0.00390625 * np.random.randint(1, 3, (1,)))}


def reference(q_rot, k_rot, v, gamma):
    q, k, g = f64(q_rot), f64(k_rot), f64(gamma)[0]
    vq = mxq(f64(v), 1, "e4m3")
    pos = np.arange(S)
    out = []
    for i in range(S // C):
        lo, hi = i * C, (i + 1) * C
        diff = pos[lo:hi, None] - pos[None, :hi]
        causal = diff >= 0
        decay = np.where(causal, g ** np.where(causal, diff, 0), 0.0)
        scores = q[:, lo:hi] @ k[:, :hi].transpose(0, 2, 1)
        p = scores * decay[None]
        out.append(mxq(p, 2, "e4m3") @ vq[:, :hi])
    return np.concatenate(out, axis=1)

@@ -1,0 +1,270 @@
+from contextlib import ExitStack
+
+import concourse.mybir as mybir
+from concourse.masks import make_identity
+
+F32 = mybir.dt.float32
+BF16 = mybir.dt.bfloat16
+U32 = mybir.dt.uint32
+U8 = mybir.dt.uint8
+FP8X4 = mybir.dt.float8_e4m3fn_x4
+MULT = mybir.AluOpType.mult
+ADD = mybir.AluOpType.add
+
+B, S, D = 8, 512, 256
+P = 128
+NCH = S // P
+FLOPS = 4 * B * S * S * D
+NG = 2
+
+
+def tile_retention_pa_kernel(tc, q_rot, k_rot, v, gamma, out):
+    nc = tc.nc
+    with ExitStack() as ctx:
+        const = ctx.enter_context(tc.tile_pool(name="const", bufs=1))
+        inp = ctx.enter_context(tc.tile_pool(name="inp", bufs=1))
+        work2 = ctx.enter_context(tc.tile_pool(name="work2", bufs=2))
+        work4 = ctx.enter_context(tc.tile_pool(name="work4", bufs=4))
+        outp = ctx.enter_context(tc.tile_pool(name="outp", bufs=2 * B))
+        psum = ctx.enter_context(tc.psum_pool(name="psum", bufs=1))
+        ctx.enter_context(tc.manual_schedule())
+
+        gam_bf = const.tile([P, 1], BF16, name="gam_bf")
+        nc.scalar.dma_start(out=gam_bf[:], in_=gamma.partition_broadcast(P))
+        q_sb, k_sb, v_sb = {}, {}, {}
+
+        def load(kind, b):
+            if kind == "v":
+                t2 = inp.tile([P, 2, NCH, D], BF16, name="v_sb%d" % b)
+                for i in range(2):
+                    nc.sync.dma_start(
+                        out=t2[:, i, :, :], in_=v[b + i].rearrange("(p t) d -> p t d", t=NCH)
+                    )
+                v_sb[b] = t2[:, 0]
+                v_sb[b + 1] = t2[:, 1]
+                return
+            t1 = inp.tile([P, NCH, D], BF16, name="%s_sb%d" % (kind, b))
+            if kind == "k":
+                nc.sync.dma_start(out=t1[:], in_=k_rot[b].rearrange("(p j) d -> p j d", j=NCH))
+                k_sb[b] = t1
+            else:
+                nc.sync.dma_start(out=t1[:], in_=q_rot[b].rearrange("(p j) d -> p j d", j=NCH))
+                q_sb[b] = t1
+
+        load("k", 0)
+        load("q", 0)
+        for b in range(0, B, 2):
+            load("v", b)
+            for bb in (b + 1, b + 2):
+                if bb < B:
+                    load("k", bb)
+                    load("q", bb)
+
+        idz = const.tile([P, P], F32, name="idz")
+        make_identity(nc, idz[:])
+        ident = idz[:]
+        GW = NCH * P * NCH
+        VW = D * NCH
+        even = const.tile([P, GW], BF16, name="even", align_bytes=64)
+        odd = const.tile([P, GW + 2 * VW], BF16, name="odd", align_bytes=64)
+        first_v = const.tile([P, 2 * VW], BF16, name="first_v", align_bytes=64)
+        grouped = [
+            t[:, 0:GW].rearrange("p (c r j) -> p c r j", c=NCH, r=P) for t in (even, odd)
+        ]
+        gam = const.tile([P, 1], F32, name="gam")
+        imp = const.tile([P, S], F32, name="imp")
+        nc.vector.memset(imp[:], 0.0)
+        wt = const.tile([P, NCH, S], F32, name="wt")
+        nc.gpsimd.memset(wt[:, 1:NCH, 0:NCH], 0.0)
+        nc.vector.tensor_copy(out=gam[:], in_=gam_bf[:])
+        nc.vector.tensor_copy(out=imp[:].rearrange("p (x s) -> p x s", s=NCH)[:, :, 0], in_=ident)
+        nc.vector.tensor_tensor_scan(
+            out=wt[:, 0, :], data0=gam[:, 0:1].to_broadcast([P, S]), data1=imp[:],
+            initial=0.0, op0=MULT, op1=ADD,
+        )
+        for t in range(1, NCH):
+            nc.vector.tensor_copy(out=wt[:, t, t:S], in_=wt[:, 0, 0 : S - t])
+        dec = const.tile([P, S, NCH], F32, name="dec")
+        for c in (2, 1, 3, 0):
+            nc.vector.tensor_copy(
+                out=dec[:, c * P : (c + 1) * P, :],
+                in_=wt[:, :, c * P : (c + 1) * P].rearrange("p t r -> p r t"),
+            )
+
+        qT, kT, scs, s0s, vcs, vss, pcs, pss = {}, {}, {}, {}, {}, {}, {}, {}
+
+        def ok(b):
+            return 0 <= b < B
+
+        def transpose(b, kind):
+            if not ok(b):
+                return
+            src, dst = (k_sb, kT) if kind == "k" else (q_sb, qT)
+            tp = psum.tile([P, NCH, P], F32, name="tp_" + kind)
+            for j in range(NCH):
+                nc.tensor.transpose(tp[:, j, :], src[b][:, j, :].bitcast(F32), ident)
+            t = work4.tile([P, S], F32, name=kind + "T")
+            if kind == "k":
+                nc.scalar.copy(out=t[:], in_=tp[:].rearrange("w j p -> w (j p)"))
+            else:
+                nc.scalar.copy(out=t[:].rearrange("w (p j) -> w p j", j=NCH), in_=tp[:].rearrange("w j p -> w p j"))
+            dst[b] = t[:].bitcast(BF16).rearrange("w (n e) -> w n e", e=2)
+
+        def score_chunk(b, sc, c):
+            for t in range(NCH):
+                for e in range(2):
+                    nc.tensor.matmul(
+                        sc[:, t, :],
+                        lhsT=kT[b][:, t * P : (t + 1) * P, e],
+                        rhs=qT[b][:, c * P : (c + 1) * P, e],
+                        start=(e == 0), stop=(e == 1),
+                    )
+
+        def scores(b, c):
+            if not ok(b):
+                return
+            sc = psum.tile([P, NCH, P], F32, name="sc%d" % c)
+            score_chunk(b, sc, c)
+            scs[(b, c)] = sc
+
+        def decay(b, c):
+            if not ok(b):
+                return
+            nc.vector.tensor_tensor(
+                out=grouped[b % NG][:, c, :, :],
+                in0=scs[(b, c)][:].rearrange("p t r -> p r t"),
+                in1=dec[:, c * P : (c + 1) * P, :],
+                op=MULT,
+            )
+
+        def scores0(b):
+            if not ok(b):
+                return
+            sc = psum.tile([P, NCH, P], F32, name="sc0")
+            score_chunk(b, sc, 0)
+            s0 = work2.tile([P, NCH, P], F32, name="s0")
+            nc.scalar.copy(out=s0[:], in_=sc[:])
+            s0s[b] = s0
+
+        def decay0(b):
+            if not ok(b):
+                return
+            nc.gpsimd.tensor_tensor(
+                out=grouped[b % NG][:, 0, :, :],
+                in0=s0s[b][:].rearrange("p t r -> p r t"),
+                in1=dec[:, 0:P, :],
+                op=MULT,
+            )
+
+        def regroup_v(b):
+            if not ok(b):
+                return
+            if b < 2:
+                vg = first_v[:, b * VW : (b + 1) * VW]
+            else:
+                vg = odd[:, GW + (b % 2) * VW : GW + (b % 2 + 1) * VW]
+            nc.vector.tensor_copy(
+                out=vg.rearrange("p (c i t) -> p c t i", i=4, t=NCH),
+                in_=v_sb[b].rearrange("p t (c i) -> p c t i", i=4),
+            )
+
+        def quantise_first_v():
+            vc = const.tile([P, 2 * D], U32, name="vc01", align_bytes=64)
+            vs = const.tile([P, 2 * D], U8, name="vs01", align_bytes=64)
+            nc.vector.quantize_mx(out=vc[:].bitcast(FP8X4), scales=vs[:], in_=first_v[:])
+            for b in range(2):
+                vcs[b], vss[b] = vc[:, b * D : (b + 1) * D], vs[:, b * D : (b + 1) * D]
+
+        def quantise_p(b, c0, c1, with_v):
+            width = S + 2 * D if b % 2 else S
+            if c0 == 0:
+                pcs[b] = work2.tile([P, width], U32, name="pc%d" % (b % 2), align_bytes=64)
+                pss[b] = work2.tile([P, width], U8, name="ps%d" % (b % 2), align_bytes=64)
+            src = odd if b % 2 else even
+            lo, hi = c0 * P, c1 * P
+            if with_v:
+                hi = width
+                for i in range(2):
+                    vcs[b + 1 + i] = pcs[b][:, S + i * D : S + (i + 1) * D]
+                    vss[b + 1 + i] = pss[b][:, S + i * D : S + (i + 1) * D]
+            nc.vector.quantize_mx(
+                out=pcs[b][:, lo:hi].bitcast(FP8X4), scales=pss[b][:, lo:hi],
+                in_=src[:, NCH * lo : NCH * hi],
+            )
+
+        def mx_pass(b, c, dst):
+            nc.tensor.matmul_mx(
+                dst,
+                lhsT=pcs[b][:, c * P : (c + 1) * P].bitcast(FP8X4),
+                lhsT_scale=pss[b][:, c * P : (c + 1) * P],
+                rhs=vcs[b].bitcast(FP8X4),
+                rhs_scale=vss[b],
+                start=True, stop=True,
+            )
+
+        def second_matmul_half(b, h):
+            o = psum.tile([P, 2, D], F32, name="o%d" % h)
+            for i in range(2):
+                mx_pass(b, 2 * h + i, o[:, i, :])
+            ot = outp.tile([P, 2, D], F32, name="ot")
+            nc.scalar.copy(out=ot[:], in_=o[:])
+            nc.sync.dma_start(
+                out=out[b, 2 * h * P : (2 * h + 2) * P, :].rearrange("(c r) d -> r c d", r=P),
+                in_=ot[:],
+            )
+
+        transpose(0, "k")
+        transpose(0, "q")
+        regroup_v(0)
+        regroup_v(1)
+        scores(0, 2)
+        scores0(0)
+        decay0(0)
+        scores(0, 1)
+        scores(0, 3)
+        transpose(1, "k")
+        transpose(1, "q")
+        scores0(1)
+        decay0(1)
+        transpose(2, "k")
+        transpose(2, "q")
+        for k in range(B):
+            last = k == B - 1
+            if ok(k - 1):
+                second_matmul_half(k - 1, 0)
+                second_matmul_half(k - 1, 1)
+            decay(k, 2)
+            scores(k + 1, 2)
+            decay(k, 1)
+            if last:
+                quantise_p(k, 0, 2, False)
+            scores(k + 1, 1)
+            decay(k, 3)
+            scores(k + 1, 3)
+            scores0(k + 2)
+            transpose(k + 3, "k")
+            transpose(k + 3, "q")
+            if k == 0:
+                quantise_first_v()
+                quantise_p(k, 0, 4, False)
+                regroup_v(2)
+            else:
+                regroup_v(k + 2)
+                if last:
+                    second_matmul_half(k, 0)
+                    quantise_p(k, 2, 4, False)
+                else:
+                    quantise_p(k, 0, 4, k % 2 == 1)
+            decay0(k + 2)
+
+        b = B - 1
+        o_a = psum.tile([P, D], F32, name="o1")
+        mx_pass(b, 2, o_a[:])
+        o_b = psum.tile([P, D], F32, name="o0")
+        mx_pass(b, 3, o_b[:])
+        ot_a = work4.tile([P, D], F32, name="ot_a")
+        nc.scalar.copy(out=ot_a[:], in_=o_a[:])
+        nc.sync.dma_start(out=out[b, 2 * P : 3 * P, :], in_=ot_a[:])
+        ot_b = work4.tile([P, D], F32, name="ot_b")
+        nc.vector.tensor_copy(out=ot_b[:], in_=o_b[:])
+        nc.sync.dma_start(out=out[b, 3 * P : 4 * P, :], in_=ot_b[:])

@@ -6,6 +6,7 @@ from concourse.masks import make_identity
 F32 = mybir.dt.float32
 BF16 = mybir.dt.bfloat16
 U32 = mybir.dt.uint32
+I32 = mybir.dt.int32
 U8 = mybir.dt.uint8
 FP8X4 = mybir.dt.float8_e4m3fn_x4
 MULT = mybir.AluOpType.mult
@@ -14,8 +15,8 @@ ADD = mybir.AluOpType.add
 B, S, D = 8, 512, 256
 P = 128
 NCH = S // P
+H = S // 2
 FLOPS = 4 * B * S * S * D
-NG = 2
 
 
 def tile_retention_pa_kernel(tc, q_rot, k_rot, v, gamma, out):
@@ -29,72 +30,79 @@ def tile_retention_pa_kernel(tc, q_rot, k_rot, v, gamma, out):
         psum = ctx.enter_context(tc.psum_pool(name="psum", bufs=1))
         ctx.enter_context(tc.manual_schedule())
 
+        def ok(b):
+            return 0 <= b < B
+
         gam_bf = const.tile([P, 1], BF16, name="gam_bf")
         nc.scalar.dma_start(out=gam_bf[:], in_=gamma.partition_broadcast(P))
         q_sb, k_sb, v_sb = {}, {}, {}
 
         def load(kind, b):
-            if kind == "v":
-                t2 = inp.tile([P, 2, NCH, D], BF16, name="v_sb%d" % b)
-                for i in range(2):
-                    nc.sync.dma_start(
-                        out=t2[:, i, :, :], in_=v[b + i].rearrange("(p t) d -> p t d", t=NCH)
-                    )
-                v_sb[b] = t2[:, 0]
-                v_sb[b + 1] = t2[:, 1]
+            if not ok(b):
                 return
+            src, dst = {"k": (k_rot, k_sb), "q": (q_rot, q_sb), "v": (v, v_sb)}[kind]
             t1 = inp.tile([P, NCH, D], BF16, name="%s_sb%d" % (kind, b))
-            if kind == "k":
-                nc.sync.dma_start(out=t1[:], in_=k_rot[b].rearrange("(p j) d -> p j d", j=NCH))
-                k_sb[b] = t1
-            else:
-                nc.sync.dma_start(out=t1[:], in_=q_rot[b].rearrange("(p j) d -> p j d", j=NCH))
-                q_sb[b] = t1
+            nc.sync.dma_start(out=t1[:], in_=src[b].rearrange("(p j) d -> p j d", j=NCH))
+            dst[b] = t1
 
-        load("k", 0)
-        load("q", 0)
-        for b in range(0, B, 2):
-            load("v", b)
-            for bb in (b + 1, b + 2):
-                if bb < B:
-                    load("k", bb)
-                    load("q", bb)
+        for kind, b in (("k", 0), ("q", 0), ("v", 0), ("v", 1), ("k", 1), ("q", 1), ("k", 2), ("q", 2),
+                        ("v", 2), ("v", 3), ("k", 3), ("q", 3), ("k", 4), ("q", 4)):
+            load(kind, b)
 
         idz = const.tile([P, P], F32, name="idz")
         make_identity(nc, idz[:])
         ident = idz[:]
-        GW = NCH * P * NCH
-        VW = D * NCH
-        even = const.tile([P, GW], BF16, name="even", align_bytes=64)
-        odd = const.tile([P, GW + 2 * VW], BF16, name="odd", align_bytes=64)
-        first_v = const.tile([P, 2 * VW], BF16, name="first_v", align_bytes=64)
-        grouped = [
-            t[:, 0:GW].rearrange("p (c r j) -> p c r j", c=NCH, r=P) for t in (even, odd)
-        ]
-        gam = const.tile([P, 1], F32, name="gam")
+        imp_n = const.tile([P, H], F32, name="imp_n")
+        nc.vector.memset(imp_n[:], 0.0)
         imp = const.tile([P, S], F32, name="imp")
         nc.vector.memset(imp[:], 0.0)
         wt = const.tile([P, NCH, S], F32, name="wt")
-        nc.gpsimd.memset(wt[:, 1:NCH, 0:NCH], 0.0)
-        nc.vector.tensor_copy(out=gam[:], in_=gam_bf[:])
+        turned = []
+        for i in range(2):
+            t1 = const.tile([P, 2, P, 2], BF16, name="turned%d" % i)
+            nc.gpsimd.memset(t1[:, :, 96:P, :], 0.0)
+            turned.append(t1)
+        v2c, v2s, vms = [], [], []
+        for g in range(B // 2):
+            c1 = const.tile([P, 2 * D], U32, name="v2c%d" % g, align_bytes=64)
+            s1 = const.tile([P, 2 * D], U8, name="v2s%d" % g, align_bytes=64)
+            m1 = const.tile([P, 2 * D], U8, name="vm%d" % g, align_bytes=64)
+            nc.gpsimd.memset(c1[:].bitcast(I32), 0)
+            nc.gpsimd.memset(s1[:].bitcast(I32), 0)
+            nc.gpsimd.memset(m1[:].bitcast(I32), 0)
+            v2c.append(c1)
+            v2s.append(s1)
+            vms.append(m1)
+        gam = const.tile([P, 1], F32, name="gam")
+        nc.vector.tensor_copy(out=imp_n[:, 0:P], in_=ident[:, ::-1])
         nc.vector.tensor_copy(out=imp[:].rearrange("p (x s) -> p x s", s=NCH)[:, :, 0], in_=ident)
+        nc.vector.tensor_copy(out=gam[:], in_=gam_bf[:])
+        w_n = const.tile([P, H], F32, name="w_n")
+        nc.vector.tensor_tensor_scan(
+            out=w_n[:], data0=gam[:, 0:1].to_broadcast([P, H]), data1=imp_n[:],
+            initial=0.0, op0=MULT, op1=ADD,
+        )
+        dec_n = const.tile([P, 2, 96, 2], F32, name="dec_n")
+        back = w_n[:, ::-1].rearrange("n (p u e) -> n u p e", u=2, e=2)
+        nc.vector.tensor_copy(out=dec_n[:, :, 0:64, :], in_=back)
+        nc.vector.tensor_copy(out=dec_n[:, :, 64:96, :], in_=dec_n[:, :, 32:64, :])
         nc.vector.tensor_tensor_scan(
             out=wt[:, 0, :], data0=gam[:, 0:1].to_broadcast([P, S]), data1=imp[:],
             initial=0.0, op0=MULT, op1=ADD,
         )
         for t in range(1, NCH):
-            nc.vector.tensor_copy(out=wt[:, t, t:S], in_=wt[:, 0, 0 : S - t])
-        dec = const.tile([P, S, NCH], F32, name="dec")
-        for c in (2, 1, 3, 0):
+            nc.vector.tensor_copy(out=wt[:, t, H:S], in_=wt[:, 0, H - t : S - t])
+        dec = const.tile([P, H, NCH], F32, name="dec")
+
+        def decay_table(c):
             nc.vector.tensor_copy(
-                out=dec[:, c * P : (c + 1) * P, :],
+                out=dec[:, (c - 2) * P : (c - 1) * P, :],
                 in_=wt[:, :, c * P : (c + 1) * P].rearrange("p t r -> p r t"),
             )
 
-        qT, kT, scs, s0s, vcs, vss, pcs, pss = {}, {}, {}, {}, {}, {}, {}, {}
-
-        def ok(b):
-            return 0 <= b < B
+        qT, kT, scs = {}, {}, {}
+        g01, g23, p01, p23 = {}, {}, {}, {}
+        vg, vcs, vss = {}, {}, {}
 
         def transpose(b, kind):
             if not ok(b):
@@ -106,103 +114,131 @@ def tile_retention_pa_kernel(tc, q_rot, k_rot, v, gamma, out):
             t = work4.tile([P, S], F32, name=kind + "T")
             if kind == "k":
                 nc.scalar.copy(out=t[:], in_=tp[:].rearrange("w j p -> w (j p)"))
+                dst[b] = t[:].bitcast(BF16).rearrange("w (j p e) -> w j p e", j=NCH, e=2)
             else:
                 nc.scalar.copy(out=t[:].rearrange("w (p j) -> w p j", j=NCH), in_=tp[:].rearrange("w j p -> w p j"))
-            dst[b] = t[:].bitcast(BF16).rearrange("w (n e) -> w n e", e=2)
-
-        def score_chunk(b, sc, c):
-            for t in range(NCH):
-                for e in range(2):
-                    nc.tensor.matmul(
-                        sc[:, t, :],
-                        lhsT=kT[b][:, t * P : (t + 1) * P, e],
-                        rhs=qT[b][:, c * P : (c + 1) * P, e],
-                        start=(e == 0), stop=(e == 1),
-                    )
+                dst[b] = t[:].bitcast(BF16).rearrange("w (n e) -> w n e", e=2)
 
         def scores(b, c):
             if not ok(b):
                 return
             sc = psum.tile([P, NCH, P], F32, name="sc%d" % c)
-            score_chunk(b, sc, c)
+            for t in range(NCH):
+                for e in range(2):
+                    nc.tensor.matmul(
+                        sc[:, t, :],
+                        lhsT=kT[b][:, t, :, e],
+                        rhs=qT[b][:, c * P : (c + 1) * P, e],
+                        start=(e == 0), stop=(e == 1),
+                    )
             scs[(b, c)] = sc
 
-        def decay(b, c):
+        def scores01(b):
             if not ok(b):
                 return
+            sc = psum.tile([P, NCH, 96], F32, name="sc01")
+            for c, lo, hi in ((1, 0, 64), (0, 64, 96)):
+                for e in range(2):
+                    nc.tensor.matmul(
+                        sc[:, :, lo:hi],
+                        lhsT=qT[b][:, c * P : (c + 1) * P, e],
+                        rhs=kT[b][:, :, 0 : hi - lo, e],
+                        start=(e == 0), stop=(e == 1),
+                    )
+            scs[(b, 0)] = sc
+
+        def decay(b, c):
+            if c == 2:
+                g23[b] = work2.tile([P, 2, P, NCH], BF16, name="g23", align_bytes=64)
             nc.vector.tensor_tensor(
-                out=grouped[b % NG][:, c, :, :],
+                out=g23[b][:, c - 2, :, :],
                 in0=scs[(b, c)][:].rearrange("p t r -> p r t"),
-                in1=dec[:, c * P : (c + 1) * P, :],
+                in1=dec[:, (c - 2) * P : (c - 1) * P, :],
                 op=MULT,
             )
 
-        def scores0(b):
-            if not ok(b):
-                return
-            sc = psum.tile([P, NCH, P], F32, name="sc0")
-            score_chunk(b, sc, 0)
-            s0 = work2.tile([P, NCH, P], F32, name="s0")
-            nc.scalar.copy(out=s0[:], in_=sc[:])
-            s0s[b] = s0
-
-        def decay0(b):
-            if not ok(b):
-                return
-            nc.gpsimd.tensor_tensor(
-                out=grouped[b % NG][:, 0, :, :],
-                in0=s0s[b][:].rearrange("p t r -> p r t"),
-                in1=dec[:, 0:P, :],
+        def decay01(b):
+            nc.vector.tensor_tensor(
+                out=turned[b % 2][:, :, 0:96, :],
+                in0=scs[(b, 0)][:].rearrange("n (u e) p -> n u p e", u=2),
+                in1=dec_n[:],
                 op=MULT,
+            )
+
+        def turn01(b):
+            pt = psum.tile([P, 2, P], F32, name="pt")
+            for u in range(2):
+                nc.tensor.transpose(
+                    pt[:, u, :], turned[b % 2][:, u, :, :].rearrange("n p e -> n (p e)").bitcast(F32), ident
+                )
+            g01[b] = work2.tile([P, P * NCH], BF16, name="g01", align_bytes=64)
+            nc.scalar.copy(
+                out=g01[b][:].bitcast(F32).rearrange("p (n u) -> p n u", u=2),
+                in_=pt[:].rearrange("p u n -> p n u"),
+            )
+
+        def quantise01(b):
+            c1 = work2.tile([P, P], U32, name="pc01", align_bytes=64)
+            s1 = work2.tile([P, P], U8, name="ps01", align_bytes=64)
+            nc.vector.quantize_mx(out=c1[:].bitcast(FP8X4), scales=s1[:], in_=g01[b][:])
+            p01[b] = (c1, s1)
+
+        def quantise23(b, c0, c1):
+            if c0 == 2:
+                pc = work2.tile([P, H], U32, name="pc23", align_bytes=64)
+                ps = work2.tile([P, H], U8, name="ps23", align_bytes=64)
+                p23[b] = (pc, ps)
+            pc, ps = p23[b]
+            lo, hi = (c0 - 2) * P, (c1 - 2) * P
+            nc.vector.quantize_mx(
+                out=pc[:, lo:hi].bitcast(FP8X4), scales=ps[:, lo:hi],
+                in_=g23[b][:].rearrange("p c r t -> p (c r t)")[:, NCH * lo : NCH * hi],
             )
 
         def regroup_v(b):
             if not ok(b):
                 return
-            if b < 2:
-                vg = first_v[:, b * VW : (b + 1) * VW]
+            if b // 2 not in vg:
+                vg[b // 2] = work2.tile([P, 2, D * NCH], BF16, name="vg", align_bytes=64)
+            o = vg[b // 2][:, b % 2, :].rearrange("p (c i t) -> p c t i", i=4, t=NCH)
+            i = v_sb[b][:].rearrange("p t (c i) -> p c t i", i=4)
+            if b % 2 == 0:
+                nc.vector.tensor_copy(out=o, in_=i)
             else:
-                vg = odd[:, GW + (b % 2) * VW : GW + (b % 2 + 1) * VW]
-            nc.vector.tensor_copy(
-                out=vg.rearrange("p (c i t) -> p c t i", i=4, t=NCH),
-                in_=v_sb[b].rearrange("p t (c i) -> p c t i", i=4),
-            )
+                nc.gpsimd.tensor_scalar(out=o, in0=i, scalar1=1.0, scalar2=0.0, op0=MULT, op1=ADD)
 
-        def quantise_first_v():
-            vc = const.tile([P, 2 * D], U32, name="vc01", align_bytes=64)
-            vs = const.tile([P, 2 * D], U8, name="vs01", align_bytes=64)
-            nc.vector.quantize_mx(out=vc[:].bitcast(FP8X4), scales=vs[:], in_=first_v[:])
-            for b in range(2):
-                vcs[b], vss[b] = vc[:, b * D : (b + 1) * D], vs[:, b * D : (b + 1) * D]
-
-        def quantise_p(b, c0, c1, with_v):
-            width = S + 2 * D if b % 2 else S
-            if c0 == 0:
-                pcs[b] = work2.tile([P, width], U32, name="pc%d" % (b % 2), align_bytes=64)
-                pss[b] = work2.tile([P, width], U8, name="ps%d" % (b % 2), align_bytes=64)
-            src = odd if b % 2 else even
-            lo, hi = c0 * P, c1 * P
-            if with_v:
-                hi = width
-                for i in range(2):
-                    vcs[b + 1 + i] = pcs[b][:, S + i * D : S + (i + 1) * D]
-                    vss[b + 1 + i] = pss[b][:, S + i * D : S + (i + 1) * D]
+        def quantise_v(g):
+            if not 0 <= g < B // 2:
+                return
+            vc = const.tile([P, 2 * D], U32, name="vc%d" % g, align_bytes=64)
+            vs = const.tile([P, 2 * D], U8, name="vs%d" % g, align_bytes=64)
             nc.vector.quantize_mx(
-                out=pcs[b][:, lo:hi].bitcast(FP8X4), scales=pss[b][:, lo:hi],
-                in_=src[:, NCH * lo : NCH * hi],
+                out=vc[:].bitcast(FP8X4), scales=vs[:], in_=vg[g][:].rearrange("p b x -> p (b x)")
             )
+            nc.sync.dma_start(out=v2c[g][64:96, :].bitcast(I32), in_=vc[0:32, :].bitcast(I32))
+            nc.sync.dma_start(out=v2s[g][64:68, :].bitcast(I32), in_=vs[0:4, :].bitcast(I32))
+            for r in (0, 32):
+                nc.sync.dma_start(out=vms[g][r : r + 4, :].bitcast(I32), in_=vs[r : r + 4, :].bitcast(I32))
+            vcs[g], vss[g] = vc, vs
 
         def mx_pass(b, c, dst):
+            g, cols = b // 2, slice((b % 2) * D, (b % 2 + 1) * D)
+            if c < 2:
+                pc, ps, pcols = p01[b][0], p01[b][1], slice(0, P)
+            else:
+                pc, ps, pcols = p23[b][0], p23[b][1], slice((c - 2) * P, (c - 1) * P)
+            vc = v2c[g] if c == 0 else vcs[g]
+            vs = (v2s[g], vms[g], vss[g], vss[g])[c]
             nc.tensor.matmul_mx(
                 dst,
-                lhsT=pcs[b][:, c * P : (c + 1) * P].bitcast(FP8X4),
-                lhsT_scale=pss[b][:, c * P : (c + 1) * P],
-                rhs=vcs[b].bitcast(FP8X4),
-                rhs_scale=vss[b],
+                lhsT=pc[:, pcols].bitcast(FP8X4), lhsT_scale=ps[:, pcols],
+                rhs=vc[:, cols].bitcast(FP8X4), rhs_scale=vs[:, cols],
                 start=True, stop=True,
             )
 
         def second_matmul_half(b, h):
+            if not ok(b):
+                return
             o = psum.tile([P, 2, D], F32, name="o%d" % h)
             for i in range(2):
                 mx_pass(b, 2 * h + i, o[:, i, :])
@@ -215,56 +251,61 @@ def tile_retention_pa_kernel(tc, q_rot, k_rot, v, gamma, out):
 
         transpose(0, "k")
         transpose(0, "q")
-        regroup_v(0)
-        regroup_v(1)
-        scores(0, 2)
-        scores0(0)
-        decay0(0)
-        scores(0, 1)
-        scores(0, 3)
         transpose(1, "k")
+        scores01(0)
+        regroup_v(1)
+        decay_table(2)
         transpose(1, "q")
-        scores0(1)
-        decay0(1)
+        scores(0, 2)
+        scores(0, 3)
         transpose(2, "k")
         transpose(2, "q")
         for k in range(B):
             last = k == B - 1
-            if ok(k - 1):
-                second_matmul_half(k - 1, 0)
-                second_matmul_half(k - 1, 1)
+            second_matmul_half(k - 1, 1)
+            decay01(k)
+            turn01(k)
+            scores01(k + 1)
+            if k == 0:
+                decay_table(3)
             decay(k, 2)
             scores(k + 1, 2)
-            decay(k, 1)
-            if last:
-                quantise_p(k, 0, 2, False)
-            scores(k + 1, 1)
+            second_matmul_half(k - 1, 0)
+            if k == 0:
+                regroup_v(0)
             decay(k, 3)
             scores(k + 1, 3)
-            scores0(k + 2)
             transpose(k + 3, "k")
             transpose(k + 3, "q")
+            if last:
+                quantise23(k, 2, 3)
+            quantise01(k)
+            if k % 2 == 0:
+                load("v", k + 4)
+                load("v", k + 5)
+            load("k", k + 5)
+            load("q", k + 5)
             if k == 0:
-                quantise_first_v()
-                quantise_p(k, 0, 4, False)
-                regroup_v(2)
-            else:
+                quantise_v(0)
+                regroup_v(3)
+            if k % 2 == 0:
                 regroup_v(k + 2)
-                if last:
-                    second_matmul_half(k, 0)
-                    quantise_p(k, 2, 4, False)
-                else:
-                    quantise_p(k, 0, 4, k % 2 == 1)
-            decay0(k + 2)
+                regroup_v(k + 5)
+            else:
+                quantise_v((k + 1) // 2)
+            if not last:
+                quantise23(k, 2, 4)
 
         b = B - 1
         o_a = psum.tile([P, D], F32, name="o1")
         mx_pass(b, 2, o_a[:])
-        o_b = psum.tile([P, D], F32, name="o0")
-        mx_pass(b, 3, o_b[:])
         ot_a = work4.tile([P, D], F32, name="ot_a")
         nc.scalar.copy(out=ot_a[:], in_=o_a[:])
         nc.sync.dma_start(out=out[b, 2 * P : 3 * P, :], in_=ot_a[:])
+        second_matmul_half(b, 0)
+        quantise23(b, 3, 4)
+        o_b = psum.tile([P, D], F32, name="sc2")
+        mx_pass(b, 3, o_b[:])
         ot_b = work4.tile([P, D], F32, name="ot_b")
         nc.vector.tensor_copy(out=ot_b[:], in_=o_b[:])
         nc.sync.dma_start(out=out[b, 3 * P : 4 * P, :], in_=ot_b[:])

@@ -45,9 +45,10 @@ def tile_retention_pa_kernel(tc, q_rot, k_rot, v, gamma, out):
             nc.sync.dma_start(out=t1[:], in_=src[b].rearrange("(p j) d -> p j d", j=NCH))
             dst[b] = t1
 
-        for kind, b in (("k", 0), ("q", 0), ("v", 0), ("v", 1), ("k", 1), ("q", 1), ("k", 2), ("q", 2),
-                        ("v", 2), ("v", 3), ("k", 3), ("q", 3), ("k", 4), ("q", 4)):
+        for kind, b in (("k", 0), ("q", 0), ("k", 1), ("q", 1), ("v", 0), ("v", 1), ("k", 2), ("q", 2),
+                        ("k", 3), ("q", 3), ("v", 2), ("v", 3), ("k", 4), ("q", 4)):
             load(kind, b)
+        LATE = (("v", 4), ("v", 5), ("k", 5), ("q", 5), ("k", 6), ("q", 6), ("v", 6), ("v", 7), ("k", 7), ("q", 7))
 
         idz = const.tile([P, P], F32, name="idz")
         make_identity(nc, idz[:])
@@ -84,14 +85,17 @@ def tile_retention_pa_kernel(tc, q_rot, k_rot, v, gamma, out):
         )
         dec_n = const.tile([P, 2, 96, 2], F32, name="dec_n")
         back = w_n[:, ::-1].rearrange("n (p u e) -> n u p e", u=2, e=2)
-        nc.vector.tensor_copy(out=dec_n[:, :, 0:64, :], in_=back)
-        nc.vector.tensor_copy(out=dec_n[:, :, 64:96, :], in_=dec_n[:, :, 32:64, :])
+        nc.scalar.copy(out=dec_n[:, :, 0:64, :], in_=back)
+        nc.scalar.copy(out=dec_n[:, :, 64:96, :], in_=back[:, :, 32:64, :])
         nc.vector.tensor_tensor_scan(
             out=wt[:, 0, :], data0=gam[:, 0:1].to_broadcast([P, S]), data1=imp[:],
             initial=0.0, op0=MULT, op1=ADD,
         )
-        for t in range(1, NCH):
-            nc.vector.tensor_copy(out=wt[:, t, H:S], in_=wt[:, 0, H - t : S - t])
+
+        def key_first_table():
+            for t in range(1, NCH):
+                nc.vector.tensor_copy(out=wt[:, t, H:S], in_=wt[:, 0, H - t : S - t])
+
         dec = const.tile([P, H, NCH], F32, name="dec")
 
         def decay_table(c):
@@ -116,7 +120,11 @@ def tile_retention_pa_kernel(tc, q_rot, k_rot, v, gamma, out):
                 nc.scalar.copy(out=t[:], in_=tp[:].rearrange("w j p -> w (j p)"))
                 dst[b] = t[:].bitcast(BF16).rearrange("w (j p e) -> w j p e", j=NCH, e=2)
             else:
-                nc.scalar.copy(out=t[:].rearrange("w (p j) -> w p j", j=NCH), in_=tp[:].rearrange("w j p -> w p j"))
+                o, i = t[:].rearrange("w (p j) -> w p j", j=NCH), tp[:].rearrange("w j p -> w p j")
+                if b == 0:
+                    nc.vector.tensor_copy(out=o, in_=i)
+                else:
+                    nc.scalar.copy(out=o, in_=i)
                 dst[b] = t[:].bitcast(BF16).rearrange("w (n e) -> w n e", e=2)
 
         def scores(b, c):
@@ -202,10 +210,10 @@ def tile_retention_pa_kernel(tc, q_rot, k_rot, v, gamma, out):
                 vg[b // 2] = work2.tile([P, 2, D * NCH], BF16, name="vg", align_bytes=64)
             o = vg[b // 2][:, b % 2, :].rearrange("p (c i t) -> p c t i", i=4, t=NCH)
             i = v_sb[b][:].rearrange("p t (c i) -> p c t i", i=4)
-            if b % 2 == 0:
-                nc.vector.tensor_copy(out=o, in_=i)
+            if b in (0, 4):
+                nc.scalar.copy(out=o, in_=i)
             else:
-                nc.gpsimd.tensor_scalar(out=o, in0=i, scalar1=1.0, scalar2=0.0, op0=MULT, op1=ADD)
+                nc.vector.tensor_copy(out=o, in_=i)
 
         def quantise_v(g):
             if not 0 <= g < B // 2:
@@ -251,61 +259,72 @@ def tile_retention_pa_kernel(tc, q_rot, k_rot, v, gamma, out):
 
         transpose(0, "k")
         transpose(0, "q")
-        transpose(1, "k")
         scores01(0)
-        regroup_v(1)
-        decay_table(2)
-        transpose(1, "q")
         scores(0, 2)
         scores(0, 3)
-        transpose(2, "k")
-        transpose(2, "q")
+        regroup_v(0)
+        transpose(1, "k")
+        transpose(1, "q")
+        key_first_table()
+        decay_table(2)
+        decay01(0)
+        decay_table(3)
+        turn01(0)
         for k in range(B):
             last = k == B - 1
-            second_matmul_half(k - 1, 1)
-            decay01(k)
-            turn01(k)
-            scores01(k + 1)
-            if k == 0:
-                decay_table(3)
             decay(k, 2)
-            scores(k + 1, 2)
-            second_matmul_half(k - 1, 0)
-            if k == 0:
-                regroup_v(0)
+            if k > 0:
+                scores(k + 1, 2)
+                second_matmul_half(k - 1, 1)
             decay(k, 3)
-            scores(k + 1, 3)
-            transpose(k + 3, "k")
-            transpose(k + 3, "q")
+            if k > 0:
+                scores(k + 1, 3)
+                second_matmul_half(k - 1, 0)
             if last:
                 quantise23(k, 2, 3)
-            quantise01(k)
-            if k % 2 == 0:
-                load("v", k + 4)
-                load("v", k + 5)
-            load("k", k + 5)
-            load("q", k + 5)
-            if k == 0:
+            elif k == 0:
+                scores01(1)
+                transpose(2, "k")
+                transpose(2, "q")
+                scores(1, 2)
+                scores(1, 3)
+                regroup_v(1)
+                quantise01(0)
                 quantise_v(0)
-                regroup_v(3)
-            if k % 2 == 0:
-                regroup_v(k + 2)
-                regroup_v(k + 5)
-            else:
-                quantise_v((k + 1) // 2)
+                for kind, b in LATE:
+                    load(kind, b)
+                quantise23(0, 2, 4)
             if not last:
+                decay01(k + 1)
+                scores01(k + 2)
+                turn01(k + 1)
+            transpose(k + 3, "k")
+            transpose(k + 3, "q")
+            if k > 0:
+                quantise01(k)
+                if k % 2 == 1:
+                    quantise_v((k + 1) // 2)
+            if k == 0:
+                regroup_v(2)
+            regroup_v(k + 3)
+            if k > 0 and not last:
                 quantise23(k, 2, 4)
 
         b = B - 1
-        o_a = psum.tile([P, D], F32, name="o1")
+        o_a = psum.tile([P, D], F32, name="tp_k")
         mx_pass(b, 2, o_a[:])
         ot_a = work4.tile([P, D], F32, name="ot_a")
         nc.scalar.copy(out=ot_a[:], in_=o_a[:])
         nc.sync.dma_start(out=out[b, 2 * P : 3 * P, :], in_=ot_a[:])
-        second_matmul_half(b, 0)
+        o_c = psum.tile([P, 2, D], F32, name="tp_q")
+        for i in range(2):
+            mx_pass(b, i, o_c[:, i, :])
         quantise23(b, 3, 4)
+        ot = outp.tile([P, 2, D], F32, name="ot")
+        nc.vector.tensor_copy(out=ot[:], in_=o_c[:])
+        nc.sync.dma_start(out=out[b, 0 : 2 * P, :].rearrange("(c r) d -> r c d", r=P), in_=ot[:])
         o_b = psum.tile([P, D], F32, name="sc2")
         mx_pass(b, 3, o_b[:])
         ot_b = work4.tile([P, D], F32, name="ot_b")
-        nc.vector.tensor_copy(out=ot_b[:], in_=o_b[:])
+        nc.scalar.copy(out=ot_b[:], in_=o_b[:])
         nc.sync.dma_start(out=out[b, 3 * P : 4 * P, :], in_=ot_b[:])

@@ -46,9 +46,9 @@ def tile_retention_pa_kernel(tc, q_rot, k_rot, v, gamma, out):
             dst[b] = t1
 
         for kind, b in (("k", 0), ("q", 0), ("k", 1), ("q", 1), ("v", 0), ("v", 1), ("k", 2), ("q", 2),
-                        ("k", 3), ("q", 3), ("v", 2), ("v", 3), ("k", 4), ("q", 4)):
+                        ("k", 3), ("q", 3), ("v", 2), ("v", 3), ("k", 4), ("q", 4), ("v", 4), ("v", 5)):
             load(kind, b)
-        LATE = (("v", 4), ("v", 5), ("k", 5), ("q", 5), ("k", 6), ("q", 6), ("v", 6), ("v", 7), ("k", 7), ("q", 7))
+        LATE = (("k", 5), ("q", 5), ("k", 6), ("q", 6), ("v", 6), ("v", 7), ("k", 7), ("q", 7))
 
         idz = const.tile([P, P], F32, name="idz")
         make_identity(nc, idz[:])
@@ -210,7 +210,7 @@ def tile_retention_pa_kernel(tc, q_rot, k_rot, v, gamma, out):
                 vg[b // 2] = work2.tile([P, 2, D * NCH], BF16, name="vg", align_bytes=64)
             o = vg[b // 2][:, b % 2, :].rearrange("p (c i t) -> p c t i", i=4, t=NCH)
             i = v_sb[b][:].rearrange("p t (c i) -> p c t i", i=4)
-            if b in (0, 4):
+            if b in (0, 6):
                 nc.scalar.copy(out=o, in_=i)
             else:
                 nc.vector.tensor_copy(out=o, in_=i)
@@ -289,8 +289,8 @@ def tile_retention_pa_kernel(tc, q_rot, k_rot, v, gamma, out):
                 scores(1, 2)
                 scores(1, 3)
                 regroup_v(1)
-                quantise01(0)
                 quantise_v(0)
+                quantise01(0)
                 for kind, b in LATE:
                     load(kind, b)
                 quantise23(0, 2, 4)
@@ -302,11 +302,17 @@ def tile_retention_pa_kernel(tc, q_rot, k_rot, v, gamma, out):
             transpose(k + 3, "q")
             if k > 0:
                 quantise01(k)
-                if k % 2 == 1:
-                    quantise_v((k + 1) // 2)
-            if k == 0:
-                regroup_v(2)
-            regroup_v(k + 3)
+                if k == 1:
+                    regroup_v(3)
+                    quantise_v(1)
+                if k == 2:
+                    regroup_v(5)
+                    quantise_v(2)
+                if k == 4:
+                    regroup_v(7)
+                    quantise_v(3)
+            if k in (0, 1, 2):
+                regroup_v({0: 2, 1: 4, 2: 6}[k])
             if k > 0 and not last:
                 quantise23(k, 2, 4)
 

@@ -6,7 +6,6 @@ from concourse.masks import make_identity
 F32 = mybir.dt.float32
 BF16 = mybir.dt.bfloat16
 U32 = mybir.dt.uint32
-I32 = mybir.dt.int32
 U8 = mybir.dt.uint8
 FP8X4 = mybir.dt.float8_e4m3fn_x4
 MULT = mybir.AluOpType.mult
@@ -25,6 +24,7 @@ def tile_retention_pa_kernel(tc, q_rot, k_rot, v, gamma, out):
         const = ctx.enter_context(tc.tile_pool(name="const", bufs=1))
         inp = ctx.enter_context(tc.tile_pool(name="inp", bufs=1))
         work2 = ctx.enter_context(tc.tile_pool(name="work2", bufs=2))
+        work3 = ctx.enter_context(tc.tile_pool(name="work3", bufs=3))
         work4 = ctx.enter_context(tc.tile_pool(name="work4", bufs=4))
         outp = ctx.enter_context(tc.tile_pool(name="outp", bufs=2 * B))
         psum = ctx.enter_context(tc.psum_pool(name="psum", bufs=1))
@@ -45,10 +45,11 @@ def tile_retention_pa_kernel(tc, q_rot, k_rot, v, gamma, out):
             nc.sync.dma_start(out=t1[:], in_=src[b].rearrange("(p j) d -> p j d", j=NCH))
             dst[b] = t1
 
-        for kind, b in (("k", 0), ("q", 0), ("k", 1), ("q", 1), ("v", 0), ("v", 1), ("k", 2), ("q", 2),
-                        ("k", 3), ("q", 3), ("v", 2), ("v", 3), ("k", 4), ("q", 4), ("v", 4), ("v", 5)):
+        for kind, b in (("k", 0), ("q", 0), ("k", 1), ("q", 1), ("v", 0), ("v", 1)):
             load(kind, b)
-        LATE = (("k", 5), ("q", 5), ("k", 6), ("q", 6), ("v", 6), ("v", 7), ("k", 7), ("q", 7))
+        for b in range(2, B, 2):
+            for kind, i in (("k", 0), ("q", 0), ("v", 0), ("v", 1), ("k", 1), ("q", 1)):
+                load(kind, b + i)
 
         idz = const.tile([P, P], F32, name="idz")
         make_identity(nc, idz[:])
@@ -60,20 +61,10 @@ def tile_retention_pa_kernel(tc, q_rot, k_rot, v, gamma, out):
         wt = const.tile([P, NCH, S], F32, name="wt")
         turned = []
         for i in range(2):
-            t1 = const.tile([P, 2, P, 2], BF16, name="turned%d" % i)
-            nc.gpsimd.memset(t1[:, :, 96:P, :], 0.0)
+            t1 = const.tile([P, 2, 2, P, 2], BF16, name="turned%d" % i)
+            nc.gpsimd.memset(t1[:, 0, :, 32:P, :], 0.0)
+            nc.gpsimd.memset(t1[:, 1, :, 64:P, :], 0.0)
             turned.append(t1)
-        v2c, v2s, vms = [], [], []
-        for g in range(B // 2):
-            c1 = const.tile([P, 2 * D], U32, name="v2c%d" % g, align_bytes=64)
-            s1 = const.tile([P, 2 * D], U8, name="v2s%d" % g, align_bytes=64)
-            m1 = const.tile([P, 2 * D], U8, name="vm%d" % g, align_bytes=64)
-            nc.gpsimd.memset(c1[:].bitcast(I32), 0)
-            nc.gpsimd.memset(s1[:].bitcast(I32), 0)
-            nc.gpsimd.memset(m1[:].bitcast(I32), 0)
-            v2c.append(c1)
-            v2s.append(s1)
-            vms.append(m1)
         gam = const.tile([P, 1], F32, name="gam")
         nc.vector.tensor_copy(out=imp_n[:, 0:P], in_=ident[:, ::-1])
         nc.vector.tensor_copy(out=imp[:].rearrange("p (x s) -> p x s", s=NCH)[:, :, 0], in_=ident)
@@ -83,10 +74,8 @@ def tile_retention_pa_kernel(tc, q_rot, k_rot, v, gamma, out):
             out=w_n[:], data0=gam[:, 0:1].to_broadcast([P, H]), data1=imp_n[:],
             initial=0.0, op0=MULT, op1=ADD,
         )
-        dec_n = const.tile([P, 2, 96, 2], F32, name="dec_n")
-        back = w_n[:, ::-1].rearrange("n (p u e) -> n u p e", u=2, e=2)
-        nc.scalar.copy(out=dec_n[:, :, 0:64, :], in_=back)
-        nc.scalar.copy(out=dec_n[:, :, 64:96, :], in_=back[:, :, 32:64, :])
+        dec_n = const.tile([P, 2, 64, 2], F32, name="dec_n")
+        nc.scalar.copy(out=dec_n[:], in_=w_n[:, ::-1].rearrange("n (p u e) -> n u p e", u=2, e=2))
         nc.vector.tensor_tensor_scan(
             out=wt[:, 0, :], data0=gam[:, 0:1].to_broadcast([P, S]), data1=imp[:],
             initial=0.0, op0=MULT, op1=ADD,
@@ -105,7 +94,7 @@ def tile_retention_pa_kernel(tc, q_rot, k_rot, v, gamma, out):
             )
 
         qT, kT, scs = {}, {}, {}
-        g01, g23, p01, p23 = {}, {}, {}, {}
+        grouped, pcs, pss = {}, {}, {}
         vg, vcs, vss = {}, {}, {}
 
         def transpose(b, kind):
@@ -144,63 +133,59 @@ def tile_retention_pa_kernel(tc, q_rot, k_rot, v, gamma, out):
         def scores01(b):
             if not ok(b):
                 return
-            sc = psum.tile([P, NCH, 96], F32, name="sc01")
-            for c, lo, hi in ((1, 0, 64), (0, 64, 96)):
+            sc = psum.tile([P, NCH * 96], F32, name="sc01")
+            for c, n, lo in ((1, 64, 0), (0, 32, NCH * 64)):
                 for e in range(2):
                     nc.tensor.matmul(
-                        sc[:, :, lo:hi],
+                        sc[:, lo : lo + NCH * n],
                         lhsT=qT[b][:, c * P : (c + 1) * P, e],
-                        rhs=kT[b][:, :, 0 : hi - lo, e],
+                        rhs=kT[b][:, :, 0:n, e],
                         start=(e == 0), stop=(e == 1),
                     )
             scs[(b, 0)] = sc
 
+        def words(b):
+            if b not in grouped:
+                grouped[b] = work3.tile([P, NCH, P, NCH], BF16, name="grouped", align_bytes=64)
+            return grouped[b]
+
         def decay(b, c):
-            if c == 2:
-                g23[b] = work2.tile([P, 2, P, NCH], BF16, name="g23", align_bytes=64)
             nc.vector.tensor_tensor(
-                out=g23[b][:, c - 2, :, :],
+                out=words(b)[:, c, :, :],
                 in0=scs[(b, c)][:].rearrange("p t r -> p r t"),
                 in1=dec[:, (c - 2) * P : (c - 1) * P, :],
                 op=MULT,
             )
 
         def decay01(b):
-            nc.vector.tensor_tensor(
-                out=turned[b % 2][:, :, 0:96, :],
-                in0=scs[(b, 0)][:].rearrange("n (u e) p -> n u p e", u=2),
-                in1=dec_n[:],
-                op=MULT,
-            )
+            for c, n, lo in ((1, 64, 0), (0, 32, NCH * 64)):
+                nc.vector.tensor_tensor(
+                    out=turned[b % 2][:, c, :, 0:n, :],
+                    in0=scs[(b, 0)][:, lo : lo + NCH * n].rearrange("n (u e p) -> n u p e", u=2, e=2),
+                    in1=dec_n[:, :, 64 - n : 64, :],
+                    op=MULT,
+                )
 
         def turn01(b):
-            pt = psum.tile([P, 2, P], F32, name="pt")
-            for u in range(2):
-                nc.tensor.transpose(
-                    pt[:, u, :], turned[b % 2][:, u, :, :].rearrange("n p e -> n (p e)").bitcast(F32), ident
-                )
-            g01[b] = work2.tile([P, P * NCH], BF16, name="g01", align_bytes=64)
+            pt = psum.tile([P, 2, 2, P], F32, name="pt")
+            for c in range(2):
+                for u in range(2):
+                    nc.tensor.transpose(
+                        pt[:, c, u, :], turned[b % 2][:, c, u, :, :].rearrange("n p e -> n (p e)").bitcast(F32), ident
+                    )
             nc.scalar.copy(
-                out=g01[b][:].bitcast(F32).rearrange("p (n u) -> p n u", u=2),
-                in_=pt[:].rearrange("p u n -> p n u"),
+                out=words(b)[:, 0:2, :, :].rearrange("p c n t -> p (c n t)").bitcast(F32).rearrange("p (c n u) -> p c n u", c=2, u=2),
+                in_=pt[:].rearrange("p c u n -> p c n u"),
             )
 
-        def quantise01(b):
-            c1 = work2.tile([P, P], U32, name="pc01", align_bytes=64)
-            s1 = work2.tile([P, P], U8, name="ps01", align_bytes=64)
-            nc.vector.quantize_mx(out=c1[:].bitcast(FP8X4), scales=s1[:], in_=g01[b][:])
-            p01[b] = (c1, s1)
-
-        def quantise23(b, c0, c1):
-            if c0 == 2:
-                pc = work2.tile([P, H], U32, name="pc23", align_bytes=64)
-                ps = work2.tile([P, H], U8, name="ps23", align_bytes=64)
-                p23[b] = (pc, ps)
-            pc, ps = p23[b]
-            lo, hi = (c0 - 2) * P, (c1 - 2) * P
+        def quantise_p(b, c0, c1):
+            if b not in pcs:
+                pcs[b] = work2.tile([P, S], U32, name="pc", align_bytes=64)
+                pss[b] = work2.tile([P, S], U8, name="ps", align_bytes=64)
+            lo, hi = c0 * P, c1 * P
             nc.vector.quantize_mx(
-                out=pc[:, lo:hi].bitcast(FP8X4), scales=ps[:, lo:hi],
-                in_=g23[b][:].rearrange("p c r t -> p (c r t)")[:, NCH * lo : NCH * hi],
+                out=pcs[b][:, lo:hi].bitcast(FP8X4), scales=pss[b][:, lo:hi],
+                in_=words(b)[:].rearrange("p c r t -> p (c r t)")[:, NCH * lo : NCH * hi],
             )
 
         def regroup_v(b):
@@ -210,7 +195,7 @@ def tile_retention_pa_kernel(tc, q_rot, k_rot, v, gamma, out):
                 vg[b // 2] = work2.tile([P, 2, D * NCH], BF16, name="vg", align_bytes=64)
             o = vg[b // 2][:, b % 2, :].rearrange("p (c i t) -> p c t i", i=4, t=NCH)
             i = v_sb[b][:].rearrange("p t (c i) -> p c t i", i=4)
-            if b in (0, 6):
+            if b in (0, 4, 6):
                 nc.scalar.copy(out=o, in_=i)
             else:
                 nc.vector.tensor_copy(out=o, in_=i)
@@ -223,24 +208,14 @@ def tile_retention_pa_kernel(tc, q_rot, k_rot, v, gamma, out):
             nc.vector.quantize_mx(
                 out=vc[:].bitcast(FP8X4), scales=vs[:], in_=vg[g][:].rearrange("p b x -> p (b x)")
             )
-            nc.sync.dma_start(out=v2c[g][64:96, :].bitcast(I32), in_=vc[0:32, :].bitcast(I32))
-            nc.sync.dma_start(out=v2s[g][64:68, :].bitcast(I32), in_=vs[0:4, :].bitcast(I32))
-            for r in (0, 32):
-                nc.sync.dma_start(out=vms[g][r : r + 4, :].bitcast(I32), in_=vs[r : r + 4, :].bitcast(I32))
             vcs[g], vss[g] = vc, vs
 
         def mx_pass(b, c, dst):
             g, cols = b // 2, slice((b % 2) * D, (b % 2 + 1) * D)
-            if c < 2:
-                pc, ps, pcols = p01[b][0], p01[b][1], slice(0, P)
-            else:
-                pc, ps, pcols = p23[b][0], p23[b][1], slice((c - 2) * P, (c - 1) * P)
-            vc = v2c[g] if c == 0 else vcs[g]
-            vs = (v2s[g], vms[g], vss[g], vss[g])[c]
             nc.tensor.matmul_mx(
                 dst,
-                lhsT=pc[:, pcols].bitcast(FP8X4), lhsT_scale=ps[:, pcols],
-                rhs=vc[:, cols].bitcast(FP8X4), rhs_scale=vs[:, cols],
+                lhsT=pcs[b][:, c * P : (c + 1) * P].bitcast(FP8X4), lhsT_scale=pss[b][:, c * P : (c + 1) * P],
+                rhs=vcs[g][:, cols].bitcast(FP8X4), rhs_scale=vss[g][:, cols],
                 start=True, stop=True,
             )
 
@@ -272,17 +247,16 @@ def tile_retention_pa_kernel(tc, q_rot, k_rot, v, gamma, out):
         turn01(0)
         for k in range(B):
             last = k == B - 1
+            if k > 0:
+                second_matmul_half(k - 1, 1)
+                second_matmul_half(k - 1, 0)
             decay(k, 2)
             if k > 0:
                 scores(k + 1, 2)
-                second_matmul_half(k - 1, 1)
             decay(k, 3)
             if k > 0:
                 scores(k + 1, 3)
-                second_matmul_half(k - 1, 0)
-            if last:
-                quantise23(k, 2, 3)
-            elif k == 0:
+            if k == 0:
                 scores01(1)
                 transpose(2, "k")
                 transpose(2, "q")
@@ -290,45 +264,33 @@ def tile_retention_pa_kernel(tc, q_rot, k_rot, v, gamma, out):
                 scores(1, 3)
                 regroup_v(1)
                 quantise_v(0)
-                quantise01(0)
-                for kind, b in LATE:
-                    load(kind, b)
-                quantise23(0, 2, 4)
             if not last:
                 decay01(k + 1)
                 scores01(k + 2)
                 turn01(k + 1)
             transpose(k + 3, "k")
             transpose(k + 3, "q")
-            if k > 0:
-                quantise01(k)
-                if k == 1:
-                    regroup_v(3)
-                    quantise_v(1)
-                if k == 2:
-                    regroup_v(5)
-                    quantise_v(2)
-                if k == 4:
-                    regroup_v(7)
-                    quantise_v(3)
-            if k in (0, 1, 2):
-                regroup_v({0: 2, 1: 4, 2: 6}[k])
-            if k > 0 and not last:
-                quantise23(k, 2, 4)
+            for b in {0: (2,), 1: (4, 3), 3: (6, 5), 5: (7,)}.get(k, ()):
+                regroup_v(b)
+            if k % 2 == 1:
+                quantise_v((k + 1) // 2)
+            if not last:
+                quantise_p(k, 0, 4)
 
         b = B - 1
+        quantise_p(b, 0, 2)
+        quantise_p(b, 2, 4)
+        o_c = psum.tile([P, 2, D], F32, name="tp_q")
+        for i in range(2):
+            mx_pass(b, i, o_c[:, i, :])
+        ot = outp.tile([P, 2, D], F32, name="ot")
+        nc.vector.tensor_copy(out=ot[:], in_=o_c[:])
+        nc.sync.dma_start(out=out[b, 0 : 2 * P, :].rearrange("(c r) d -> r c d", r=P), in_=ot[:])
         o_a = psum.tile([P, D], F32, name="tp_k")
         mx_pass(b, 2, o_a[:])
         ot_a = work4.tile([P, D], F32, name="ot_a")
         nc.scalar.copy(out=ot_a[:], in_=o_a[:])
         nc.sync.dma_start(out=out[b, 2 * P : 3 * P, :], in_=ot_a[:])
-        o_c = psum.tile([P, 2, D], F32, name="tp_q")
-        for i in range(2):
-            mx_pass(b, i, o_c[:, i, :])
-        quantise23(b, 3, 4)
-        ot = outp.tile([P, 2, D], F32, name="ot")
-        nc.vector.tensor_copy(out=ot[:], in_=o_c[:])
-        nc.sync.dma_start(out=out[b, 0 : 2 * P, :].rearrange("(c r) d -> r c d", r=P), in_=ot[:])
         o_b = psum.tile([P, D], F32, name="sc2")
         mx_pass(b, 3, o_b[:])
         ot_b = work4.tile([P, D], F32, name="ot_b")

@@ -191,31 +191,24 @@ def tile_retention_pa_kernel(tc, q_rot, k_rot, v, gamma, out):
         def regroup_v(b):
             if not ok(b):
                 return
-            if b // 2 not in vg:
-                vg[b // 2] = work2.tile([P, 2, D * NCH], BF16, name="vg", align_bytes=64)
-            o = vg[b // 2][:, b % 2, :].rearrange("p (c i t) -> p c t i", i=4, t=NCH)
+            vg[b] = work2.tile([P, D * NCH], BF16, name="vg", align_bytes=64)
+            o = vg[b][:].rearrange("p (c i t) -> p c t i", i=4, t=NCH)
             i = v_sb[b][:].rearrange("p t (c i) -> p c t i", i=4)
-            if b in (0, 4, 6):
+            if b < 2:
                 nc.scalar.copy(out=o, in_=i)
             else:
-                nc.vector.tensor_copy(out=o, in_=i)
+                nc.gpsimd.tensor_scalar(out=o, in0=i, scalar1=1.0, scalar2=0.0, op0=MULT, op1=ADD)
 
-        def quantise_v(g):
-            if not 0 <= g < B // 2:
-                return
-            vc = const.tile([P, 2 * D], U32, name="vc%d" % g, align_bytes=64)
-            vs = const.tile([P, 2 * D], U8, name="vs%d" % g, align_bytes=64)
-            nc.vector.quantize_mx(
-                out=vc[:].bitcast(FP8X4), scales=vs[:], in_=vg[g][:].rearrange("p b x -> p (b x)")
-            )
-            vcs[g], vss[g] = vc, vs
+        def quantise_v(b):
+            vcs[b] = work2.tile([P, D], U32, name="vc", align_bytes=64)
+            vss[b] = work2.tile([P, D], U8, name="vs", align_bytes=64)
+            nc.vector.quantize_mx(out=vcs[b][:].bitcast(FP8X4), scales=vss[b][:], in_=vg[b][:])
 
         def mx_pass(b, c, dst):
-            g, cols = b // 2, slice((b % 2) * D, (b % 2 + 1) * D)
             nc.tensor.matmul_mx(
                 dst,
                 lhsT=pcs[b][:, c * P : (c + 1) * P].bitcast(FP8X4), lhsT_scale=pss[b][:, c * P : (c + 1) * P],
-                rhs=vcs[g][:, cols].bitcast(FP8X4), rhs_scale=vss[g][:, cols],
+                rhs=vcs[b][:].bitcast(FP8X4), rhs_scale=vss[b][:],
                 start=True, stop=True,
             )
 
@@ -256,28 +249,26 @@ def tile_retention_pa_kernel(tc, q_rot, k_rot, v, gamma, out):
             decay(k, 3)
             if k > 0:
                 scores(k + 1, 3)
-            if k == 0:
+            else:
                 scores01(1)
                 transpose(2, "k")
                 transpose(2, "q")
                 scores(1, 2)
                 scores(1, 3)
                 regroup_v(1)
-                quantise_v(0)
             if not last:
                 decay01(k + 1)
                 scores01(k + 2)
                 turn01(k + 1)
             transpose(k + 3, "k")
             transpose(k + 3, "q")
-            for b in {0: (2,), 1: (4, 3), 3: (6, 5), 5: (7,)}.get(k, ()):
-                regroup_v(b)
-            if k % 2 == 1:
-                quantise_v((k + 1) // 2)
             if not last:
                 quantise_p(k, 0, 4)
+                quantise_v(k)
+            regroup_v(k + 2)
 
         b = B - 1
+        quantise_v(b)
         quantise_p(b, 0, 2)
         quantise_p(b, 2, 4)
         o_c = psum.tile([P, 2, D], F32, name="tp_q")

@@ -110,10 +110,7 @@ def tile_retention_pa_kernel(tc, q_rot, k_rot, v, gamma, out):
                 dst[b] = t[:].bitcast(BF16).rearrange("w (j p e) -> w j p e", j=NCH, e=2)
             else:
                 o, i = t[:].rearrange("w (p j) -> w p j", j=NCH), tp[:].rearrange("w j p -> w p j")
-                if b == 0:
-                    nc.vector.tensor_copy(out=o, in_=i)
-                else:
-                    nc.scalar.copy(out=o, in_=i)
+                nc.scalar.copy(out=o, in_=i)
                 dst[b] = t[:].bitcast(BF16).rearrange("w (n e) -> w n e", e=2)
 
         def scores(b, c):
@@ -194,14 +191,13 @@ def tile_retention_pa_kernel(tc, q_rot, k_rot, v, gamma, out):
             vg[b] = work2.tile([P, D * NCH], BF16, name="vg", align_bytes=64)
             o = vg[b][:].rearrange("p (c i t) -> p c t i", i=4, t=NCH)
             i = v_sb[b][:].rearrange("p t (c i) -> p c t i", i=4)
-            if b < 2:
-                nc.scalar.copy(out=o, in_=i)
-            else:
-                nc.gpsimd.tensor_scalar(out=o, in0=i, scalar1=1.0, scalar2=0.0, op0=MULT, op1=ADD)
+            if b == 0:
+                nc.vector.memset(vg[b][:, 0:2], 0.0)
+            nc.gpsimd.tensor_scalar(out=o, in0=i, scalar1=1.0, scalar2=0.0, op0=MULT, op1=ADD)
 
         def quantise_v(b):
-            vcs[b] = work2.tile([P, D], U32, name="vc", align_bytes=64)
-            vss[b] = work2.tile([P, D], U8, name="vs", align_bytes=64)
+            vcs[b] = work4.tile([P, D], U32, name="vc", align_bytes=64)
+            vss[b] = work4.tile([P, D], U8, name="vs", align_bytes=64)
             nc.vector.quantize_mx(out=vcs[b][:].bitcast(FP8X4), scales=vss[b][:], in_=vg[b][:])
 
         def mx_pass(b, c, dst):
@@ -212,78 +208,78 @@ def tile_retention_pa_kernel(tc, q_rot, k_rot, v, gamma, out):
                 start=True, stop=True,
             )
 
-        def second_matmul_half(b, h):
+        def second_matmul(b, c0, c1, bank, copy):
             if not ok(b):
                 return
-            o = psum.tile([P, 2, D], F32, name="o%d" % h)
-            for i in range(2):
-                mx_pass(b, 2 * h + i, o[:, i, :])
-            ot = outp.tile([P, 2, D], F32, name="ot")
-            nc.scalar.copy(out=ot[:], in_=o[:])
+            n = c1 - c0
+            o = psum.tile([P, n, D], F32, name=bank)
+            for c in range(c0, c1):
+                mx_pass(b, c, o[:, c - c0, :])
+            ot = outp.tile([P, n, D], F32, name="ot")
+            copy(out=ot[:], in_=o[:])
             nc.sync.dma_start(
-                out=out[b, 2 * h * P : (2 * h + 2) * P, :].rearrange("(c r) d -> r c d", r=P),
+                out=out[b, c0 * P : c1 * P, :].rearrange("(c r) d -> r c d", r=P),
                 in_=ot[:],
             )
 
         transpose(0, "k")
         transpose(0, "q")
-        scores01(0)
-        scores(0, 2)
-        scores(0, 3)
-        regroup_v(0)
-        transpose(1, "k")
-        transpose(1, "q")
         key_first_table()
         decay_table(2)
-        decay01(0)
         decay_table(3)
+        regroup_v(0)
+        regroup_v(1)
+        scores01(0)
+        transpose(1, "k")
+        transpose(1, "q")
+        decay01(0)
+        scores(0, 2)
+        scores(0, 3)
         turn01(0)
-        for k in range(B):
-            last = k == B - 1
-            if k > 0:
-                second_matmul_half(k - 1, 1)
-                second_matmul_half(k - 1, 0)
+        for k in range(B - 2):
             decay(k, 2)
             if k > 0:
                 scores(k + 1, 2)
             decay(k, 3)
             if k > 0:
                 scores(k + 1, 3)
+                second_matmul(k - 1, 2, 4, "o1", nc.scalar.copy)
+                second_matmul(k - 1, 0, 2, "o0", nc.scalar.copy)
             else:
+                quantise_v(0)
+                regroup_v(2)
                 scores01(1)
                 transpose(2, "k")
                 transpose(2, "q")
                 scores(1, 2)
                 scores(1, 3)
-                regroup_v(1)
-            if not last:
-                decay01(k + 1)
-                scores01(k + 2)
-                turn01(k + 1)
+            decay01(k + 1)
+            scores01(k + 2)
+            turn01(k + 1)
             transpose(k + 3, "k")
             transpose(k + 3, "q")
-            if not last:
-                quantise_p(k, 0, 4)
-                quantise_v(k)
-            regroup_v(k + 2)
+            quantise_p(k, 0, 4)
+            quantise_v(k + 1)
+            if k + 3 < B:
+                regroup_v(k + 3)
 
-        b = B - 1
+        a, b = B - 2, B - 1
+        decay(a, 2)
+        scores(b, 2)
+        second_matmul(a - 1, 2, 4, "o1", nc.scalar.copy)
+        decay(a, 3)
+        scores(b, 3)
+        second_matmul(a - 1, 0, 2, "o0", nc.scalar.copy)
+        decay01(b)
+        turn01(b)
+        quantise_p(a, 0, 4)
+        decay(b, 2)
+        decay(b, 3)
         quantise_v(b)
         quantise_p(b, 0, 2)
         quantise_p(b, 2, 4)
-        o_c = psum.tile([P, 2, D], F32, name="tp_q")
-        for i in range(2):
-            mx_pass(b, i, o_c[:, i, :])
-        ot = outp.tile([P, 2, D], F32, name="ot")
-        nc.vector.tensor_copy(out=ot[:], in_=o_c[:])
-        nc.sync.dma_start(out=out[b, 0 : 2 * P, :].rearrange("(c r) d -> r c d", r=P), in_=ot[:])
-        o_a = psum.tile([P, D], F32, name="tp_k")
-        mx_pass(b, 2, o_a[:])
-        ot_a = work4.tile([P, D], F32, name="ot_a")
-        nc.scalar.copy(out=ot_a[:], in_=o_a[:])
-        nc.sync.dma_start(out=out[b, 2 * P : 3 * P, :], in_=ot_a[:])
-        o_b = psum.tile([P, D], F32, name="sc2")
-        mx_pass(b, 3, o_b[:])
-        ot_b = work4.tile([P, D], F32, name="ot_b")
-        nc.scalar.copy(out=ot_b[:], in_=o_b[:])
-        nc.sync.dma_start(out=out[b, 3 * P : 4 * P, :], in_=ot_b[:])
+        second_matmul(a, 2, 4, "tp_k", nc.scalar.copy)
+        second_matmul(a, 0, 2, "tp_q", nc.scalar.copy)
+        second_matmul(b, 0, 2, "sc01", nc.vector.tensor_copy)
+        second_matmul(b, 2, 3, "sc2", nc.scalar.copy)
+        second_matmul(b, 3, 4, "sc3", nc.vector.tensor_copy)

@@ -34,7 +34,7 @@ def tile_retention_pa_kernel(tc, q_rot, k_rot, v, gamma, out):
             return 0 <= b < B
 
         gam_bf = const.tile([P, 1], BF16, name="gam_bf")
-        nc.scalar.dma_start(out=gam_bf[:], in_=gamma.partition_broadcast(P))
+        nc.sync.dma_start(out=gam_bf[:], in_=gamma.partition_broadcast(P))
         q_sb, k_sb, v_sb = {}, {}, {}
 
         def load(kind, b):
@@ -75,11 +75,13 @@ def tile_retention_pa_kernel(tc, q_rot, k_rot, v, gamma, out):
             initial=0.0, op0=MULT, op1=ADD,
         )
         dec_n = const.tile([P, 2, 64, 2], F32, name="dec_n")
-        nc.scalar.copy(out=dec_n[:], in_=w_n[:, ::-1].rearrange("n (p u e) -> n u p e", u=2, e=2))
         nc.vector.tensor_tensor_scan(
             out=wt[:, 0, :], data0=gam[:, 0:1].to_broadcast([P, S]), data1=imp[:],
             initial=0.0, op0=MULT, op1=ADD,
         )
+
+        def query_first_table():
+            nc.scalar.copy(out=dec_n[:], in_=w_n[:, ::-1].rearrange("n (p u e) -> n u p e", u=2, e=2))
 
         def key_first_table():
             for t in range(1, NCH):
@@ -224,6 +226,7 @@ def tile_retention_pa_kernel(tc, q_rot, k_rot, v, gamma, out):
 
         transpose(0, "k")
         transpose(0, "q")
+        query_first_table()
         key_first_table()
         decay_table(2)
         decay_table(3)

@@ -232,8 +232,8 @@ def tile_retention_pa_kernel(tc, q_rot, k_rot, v, gamma, out):
         decay_table(3)
         regroup_v(0)
         regroup_v(1)
-        scores01(0)
         transpose(1, "k")
+        scores01(0)
         transpose(1, "q")
         decay01(0)
         scores(0, 2)
@@ -249,8 +249,6 @@ def tile_retention_pa_kernel(tc, q_rot, k_rot, v, gamma, out):
                 second_matmul(k - 1, 2, 4, "o1", nc.scalar.copy)
                 second_matmul(k - 1, 0, 2, "o0", nc.scalar.copy)
             else:
-                quantise_v(0)
-                regroup_v(2)
                 scores01(1)
                 transpose(2, "k")
                 transpose(2, "q")
@@ -262,9 +260,8 @@ def tile_retention_pa_kernel(tc, q_rot, k_rot, v, gamma, out):
             transpose(k + 3, "k")
             transpose(k + 3, "q")
             quantise_p(k, 0, 4)
-            quantise_v(k + 1)
-            if k + 3 < B:
-                regroup_v(k + 3)
+            quantise_v(k)
+            regroup_v(k + 2)
 
         a, b = B - 2, B - 1
         decay(a, 2)
@@ -276,6 +273,7 @@ def tile_retention_pa_kernel(tc, q_rot, k_rot, v, gamma, out):
         decay01(b)
         turn01(b)
         quantise_p(a, 0, 4)
+        quantise_v(a)
         decay(b, 2)
         decay(b, 3)
         quantise_v(b)

from contextlib import ExitStack

import concourse.mybir as mybir
from concourse.masks import make_identity

F32 = mybir.dt.float32
BF16 = mybir.dt.bfloat16
U32 = mybir.dt.uint32
U8 = mybir.dt.uint8
FP8X4 = mybir.dt.float8_e4m3fn_x4
MULT = mybir.AluOpType.mult
ADD = mybir.AluOpType.add

B, S, D = 8, 512, 256
P = 128
NCH = S // P
H = S // 2
FLOPS = 4 * B * S * S * D


def tile_retention_pa_kernel(tc, q_rot, k_rot, v, gamma, out):
    nc = tc.nc
    with ExitStack() as ctx:
        const = ctx.enter_context(tc.tile_pool(name="const", bufs=1))
        inp = ctx.enter_context(tc.tile_pool(name="inp", bufs=1))
        work2 = ctx.enter_context(tc.tile_pool(name="work2", bufs=2))
        work3 = ctx.enter_context(tc.tile_pool(name="work3", bufs=3))
        work4 = ctx.enter_context(tc.tile_pool(name="work4", bufs=4))
        outp = ctx.enter_context(tc.tile_pool(name="outp", bufs=2 * B))
        psum = ctx.enter_context(tc.psum_pool(name="psum", bufs=1))
        ctx.enter_context(tc.manual_schedule())

        def ok(b):
            return 0 <= b < B

        gam_bf = const.tile([P, 1], BF16, name="gam_bf")
        nc.sync.dma_start(out=gam_bf[:], in_=gamma.partition_broadcast(P))
        q_sb, k_sb, v_sb = {}, {}, {}

        def load(kind, b):
            if not ok(b):
                return
            src, dst = {"k": (k_rot, k_sb), "q": (q_rot, q_sb), "v": (v, v_sb)}[kind]
            t1 = inp.tile([P, NCH, D], BF16, name="%s_sb%d" % (kind, b))
            nc.sync.dma_start(out=t1[:], in_=src[b].rearrange("(p j) d -> p j d", j=NCH))
            dst[b] = t1

        for kind, b in (("k", 0), ("q", 0), ("k", 1), ("q", 1), ("v", 0), ("v", 1)):
            load(kind, b)
        for b in range(2, B, 2):
            for kind, i in (("k", 0), ("q", 0), ("v", 0), ("v", 1), ("k", 1), ("q", 1)):
                load(kind, b + i)

        idz = const.tile([P, P], F32, name="idz")
        make_identity(nc, idz[:])
        ident = idz[:]
        imp_n = const.tile([P, H], F32, name="imp_n")
        nc.vector.memset(imp_n[:], 0.0)
        imp = const.tile([P, S], F32, name="imp")
        nc.vector.memset(imp[:], 0.0)
        wt = const.tile([P, NCH, S], F32, name="wt")
        turned = []
        for i in range(2):
            t1 = const.tile([P, 2, 2, P, 2], BF16, name="turned%d" % i)
            nc.gpsimd.memset(t1[:, 0, :, 32:P, :], 0.0)
            nc.gpsimd.memset(t1[:, 1, :, 64:P, :], 0.0)
            turned.append(t1)
        gam = const.tile([P, 1], F32, name="gam")
        nc.vector.tensor_copy(out=imp_n[:, 0:P], in_=ident[:, ::-1])
        nc.vector.tensor_copy(out=imp[:].rearrange("p (x s) -> p x s", s=NCH)[:, :, 0], in_=ident)
        nc.vector.tensor_copy(out=gam[:], in_=gam_bf[:])
        w_n = const.tile([P, H], F32, name="w_n")
        nc.vector.tensor_tensor_scan(
            out=w_n[:], data0=gam[:, 0:1].to_broadcast([P, H]), data1=imp_n[:],
            initial=0.0, op0=MULT, op1=ADD,
        )
        dec_n = const.tile([P, 2, 64, 2], F32, name="dec_n")
        nc.vector.tensor_tensor_scan(
            out=wt[:, 0, :], data0=gam[:, 0:1].to_broadcast([P, S]), data1=imp[:],
            initial=0.0, op0=MULT, op1=ADD,
        )

        def query_first_table():
            nc.scalar.copy(out=dec_n[:], in_=w_n[:, ::-1].rearrange("n (p u e) -> n u p e", u=2, e=2))

        def key_first_table():
            for t in range(1, NCH):
                nc.vector.tensor_copy(out=wt[:, t, H:S], in_=wt[:, 0, H - t : S - t])

        dec = const.tile([P, H, NCH], F32, name="dec")

        def decay_table(c):
            nc.vector.tensor_copy(
                out=dec[:, (c - 2) * P : (c - 1) * P, :],
                in_=wt[:, :, c * P : (c + 1) * P].rearrange("p t r -> p r t"),
            )

        qT, kT, scs = {}, {}, {}
        grouped, pcs, pss = {}, {}, {}
        vg, vcs, vss = {}, {}, {}

        def transpose(b, kind):
            if not ok(b):
                return
            src, dst = (k_sb, kT) if kind == "k" else (q_sb, qT)
            tp = psum.tile([P, NCH, P], F32, name="tp_" + kind)
            for j in range(NCH):
                nc.tensor.transpose(tp[:, j, :], src[b][:, j, :].bitcast(F32), ident)
            t = work4.tile([P, S], F32, name=kind + "T")
            if kind == "k":
                nc.scalar.copy(out=t[:], in_=tp[:].rearrange("w j p -> w (j p)"))
                dst[b] = t[:].bitcast(BF16).rearrange("w (j p e) -> w j p e", j=NCH, e=2)
            else:
                o, i = t[:].rearrange("w (p j) -> w p j", j=NCH), tp[:].rearrange("w j p -> w p j")
                nc.scalar.copy(out=o, in_=i)
                dst[b] = t[:].bitcast(BF16).rearrange("w (n e) -> w n e", e=2)

        def scores(b, c):
            if not ok(b):
                return
            sc = psum.tile([P, NCH, P], F32, name="sc%d" % c)
            for t in range(NCH):
                for e in range(2):
                    nc.tensor.matmul(
                        sc[:, t, :],
                        lhsT=kT[b][:, t, :, e],
                        rhs=qT[b][:, c * P : (c + 1) * P, e],
                        start=(e == 0), stop=(e == 1),
                    )
            scs[(b, c)] = sc

        def scores01(b):
            if not ok(b):
                return
            sc = psum.tile([P, NCH * 96], F32, name="sc01")
            for c, n, lo in ((1, 64, 0), (0, 32, NCH * 64)):
                for e in range(2):
                    nc.tensor.matmul(
                        sc[:, lo : lo + NCH * n],
                        lhsT=qT[b][:, c * P : (c + 1) * P, e],
                        rhs=kT[b][:, :, 0:n, e],
                        start=(e == 0), stop=(e == 1),
                    )
            scs[(b, 0)] = sc

        def words(b):
            if b not in grouped:
                grouped[b] = work3.tile([P, NCH, P, NCH], BF16, name="grouped", align_bytes=64)
            return grouped[b]

        def decay(b, c):
            nc.vector.tensor_tensor(
                out=words(b)[:, c, :, :],
                in0=scs[(b, c)][:].rearrange("p t r -> p r t"),
                in1=dec[:, (c - 2) * P : (c - 1) * P, :],
                op=MULT,
            )

        def decay01(b):
            for c, n, lo in ((1, 64, 0), (0, 32, NCH * 64)):
                nc.vector.tensor_tensor(
                    out=turned[b % 2][:, c, :, 0:n, :],
                    in0=scs[(b, 0)][:, lo : lo + NCH * n].rearrange("n (u e p) -> n u p e", u=2, e=2),
                    in1=dec_n[:, :, 64 - n : 64, :],
                    op=MULT,
                )

        def turn01(b):
            pt = psum.tile([P, 2, 2, P], F32, name="pt")
            for c in range(2):
                for u in range(2):
                    nc.tensor.transpose(
                        pt[:, c, u, :], turned[b % 2][:, c, u, :, :].rearrange("n p e -> n (p e)").bitcast(F32), ident
                    )
            nc.scalar.copy(
                out=words(b)[:, 0:2, :, :].rearrange("p c n t -> p (c n t)").bitcast(F32).rearrange("p (c n u) -> p c n u", c=2, u=2),
                in_=pt[:].rearrange("p c u n -> p c n u"),
            )

        def quantise_p(b, c0, c1):
            if b not in pcs:
                pcs[b] = work2.tile([P, S], U32, name="pc", align_bytes=64)
                pss[b] = work2.tile([P, S], U8, name="ps", align_bytes=64)
            lo, hi = c0 * P, c1 * P
            nc.vector.quantize_mx(
                out=pcs[b][:, lo:hi].bitcast(FP8X4), scales=pss[b][:, lo:hi],
                in_=words(b)[:].rearrange("p c r t -> p (c r t)")[:, NCH * lo : NCH * hi],
            )

        def regroup_v(b):
            if not ok(b):
                return
            vg[b] = work2.tile([P, D * NCH], BF16, name="vg", align_bytes=64)
            o = vg[b][:].rearrange("p (c i t) -> p c t i", i=4, t=NCH)
            i = v_sb[b][:].rearrange("p t (c i) -> p c t i", i=4)
            if b == 0:
                nc.vector.memset(vg[b][:, 0:2], 0.0)
            nc.gpsimd.tensor_scalar(out=o, in0=i, scalar1=1.0, scalar2=0.0, op0=MULT, op1=ADD)

        def quantise_v(b):
            vcs[b] = work4.tile([P, D], U32, name="vc", align_bytes=64)
            vss[b] = work4.tile([P, D], U8, name="vs", align_bytes=64)
            nc.vector.quantize_mx(out=vcs[b][:].bitcast(FP8X4), scales=vss[b][:], in_=vg[b][:])

        def mx_pass(b, c, dst):
            nc.tensor.matmul_mx(
                dst,
                lhsT=pcs[b][:, c * P : (c + 1) * P].bitcast(FP8X4), lhsT_scale=pss[b][:, c * P : (c + 1) * P],
                rhs=vcs[b][:].bitcast(FP8X4), rhs_scale=vss[b][:],
                start=True, stop=True,
            )

        def second_matmul(b, c0, c1, bank, copy):
            if not ok(b):
                return
            n = c1 - c0
            o = psum.tile([P, n, D], F32, name=bank)
            for c in range(c0, c1):
                mx_pass(b, c, o[:, c - c0, :])
            ot = outp.tile([P, n, D], F32, name="ot")
            copy(out=ot[:], in_=o[:])
            nc.sync.dma_start(
                out=out[b, c0 * P : c1 * P, :].rearrange("(c r) d -> r c d", r=P),
                in_=ot[:],
            )

        transpose(0, "k")
        transpose(0, "q")
        query_first_table()
        key_first_table()
        decay_table(2)
        decay_table(3)
        regroup_v(0)
        regroup_v(1)
        transpose(1, "k")
        scores01(0)
        transpose(1, "q")
        decay01(0)
        scores(0, 2)
        scores(0, 3)
        turn01(0)
        for k in range(B - 2):
            decay(k, 2)
            if k > 0:
                scores(k + 1, 2)
            decay(k, 3)
            if k > 0:
                scores(k + 1, 3)
                second_matmul(k - 1, 2, 4, "o1", nc.scalar.copy)
                second_matmul(k - 1, 0, 2, "o0", nc.scalar.copy)
            else:
                scores01(1)
                transpose(2, "k")
                transpose(2, "q")
                scores(1, 2)
                scores(1, 3)
            decay01(k + 1)
            scores01(k + 2)
            turn01(k + 1)
            transpose(k + 3, "k")
            transpose(k + 3, "q")
            quantise_p(k, 0, 4)
            quantise_v(k)
            regroup_v(k + 2)

        a, b = B - 2, B - 1
        decay(a, 2)
        scores(b, 2)
        second_matmul(a - 1, 2, 4, "o1", nc.scalar.copy)
        decay(a, 3)
        scores(b, 3)
        second_matmul(a - 1, 0, 2, "o0", nc.scalar.copy)
        decay01(b)
        turn01(b)
        quantise_p(a, 0, 4)
        quantise_v(a)
        decay(b, 2)
        decay(b, 3)
        quantise_v(b)
        quantise_p(b, 0, 2)
        quantise_p(b, 2, 4)
        second_matmul(a, 2, 4, "tp_k", nc.scalar.copy)
        second_matmul(a, 0, 2, "tp_q", nc.scalar.copy)
        second_matmul(b, 0, 2, "sc01", nc.vector.tensor_copy)
        second_matmul(b, 2, 3, "sc2", nc.scalar.copy)
        second_matmul(b, 3, 4, "sc3", nc.vector.tensor_copy)
